import numpy as np
import ml_dtypes


def mxq(x, axis, fmt="e4m3"):
    dtype, down = {"e4m3": (ml_dtypes.float8_e4m3fn, 7), "e5m2": (ml_dtypes.float8_e5m2, 14)}[fmt]
    v = np.moveaxis(np.asarray(x, np.float32).astype(ml_dtypes.bfloat16).astype(np.float64), axis, -1)
    blocks = v.reshape(v.shape[:-1] + (-1, 32))
    amax = np.abs(blocks).max(-1, keepdims=True)
    byte = np.maximum(np.where(amax > 0, np.frexp(amax)[1] - 1 + 127, 0) - down, 1)
    scale = np.exp2(byte - 127.0)
    codes = (blocks / scale).astype(np.float32).astype(dtype).astype(np.float64)
    return np.moveaxis((codes * scale).reshape(v.shape), -1, axis)


WIDE = False


def mx_kscale(k):
    if not WIDE:
        return np.ones(k)
    levels = np.array([10, -10, 5, -5, 0])
    a = np.random.permutation(np.resize(levels, k // 512 * 4)).reshape(k // 512, 4)
    idx = np.arange(k)
    return np.exp2(a[idx // 512, idx % 128 // 32])


BF16 = ml_dtypes.bfloat16


def bf(x):
    return np.asarray(x, np.float32).astype(BF16)


def f64(x):
    return np.asarray(x).astype(np.float64)


B, C, H, W, K = 4, 1024, 32, 32, 128
N = H * W
XS = 1.6 / C ** 0.25
CS = 0.4 / C ** 0.25


def setup_inputs():
    s = mx_kscale(N)
    z = 1.3 * np.random.standard_normal((B, N, K)) + np.random.standard_normal((1, 1, K))
    a = np.exp(z - z.max(axis=-1, keepdims=True))
    a = a / a.sum(axis=-1, keepdims=True)
    feat = XS * (np.random.standard_normal((B, N, C)) + 0.4 * np.random.standard_normal((1, 1, C)))
    return {'assign': bf(a * s[None, :, None]),
            'xp': bf(feat / s[None, :, None]),
            'codebook': bf(np.random.standard_normal((K, C)) * CS / s.mean())}


def reference(assign, xp, codebook):
    assign, xp, codebook = f64(assign), f64(xp), f64(codebook)
    a_sum = np.sum(assign, axis=1)
    e = (mxq(assign, 1, 'e4m3').transpose(0, 2, 1) @ mxq(xp, 1, 'e4m3')) - a_sum[:, :, None] * codebook[None]
    return e

@@ -1,0 +1,165 @@
+from contextlib import ExitStack
+
+import concourse.mybir as mybir
+
+FP8X4 = mybir.dt.float8_e4m3fn_x4
+BF16 = mybir.dt.bfloat16
+F32 = mybir.dt.float32
+U32 = mybir.dt.uint32
+U8 = mybir.dt.uint8
+
+B = 4
+NPIX = 1024
+K = 128
+C = 1024
+P = 128
+PACK = 4
+PASSES = NPIX // (P * PACK)
+N_TILE = 512
+ONES = 32
+
+FLOPS = 2 * B * NPIX * K * C
+
+VECTOR_COLS = {1024: 416, 512: 208, 256: 104}
+
+
+def regroup(copy, dst, src):
+    copy(
+        out=dst.rearrange("p (c i) j -> p c j i", i=4),
+        in_=src.rearrange("p j (c i) -> p c j i", i=4),
+    )
+
+
+def tile_lvc_pb_kernel(tc, assign, xp, codebook, out):
+    nc = tc.nc
+    with ExitStack() as ctx:
+        raw = ctx.enter_context(tc.tile_pool(name="raw", bufs=1))
+        stage = ctx.enter_context(tc.tile_pool(name="stage", bufs=3))
+        keep = ctx.enter_context(tc.tile_pool(name="keep", bufs=1))
+        ps_acc = ctx.enter_context(tc.psum_pool(name="ps_acc", bufs=6))
+        ps_sum = ctx.enter_context(tc.psum_pool(name="ps_sum", bufs=2))
+
+        a_raw = []
+        for b in range(B):
+            t = raw.tile([P, PASSES, PACK, K], BF16, name="a_raw%d" % b)
+            nc.sync.dma_start(
+                out=t[:],
+                in_=assign[b, :, :].rearrange("(c p j) k -> p c j k", c=PASSES, p=P, j=PACK),
+            )
+            a_raw.append(t)
+        x_raw = {}
+        cb = raw.tile([P, C], BF16, name="cb")
+        for b in range(B):
+            for c in range(PASSES):
+                t = raw.tile([P, PACK, C], BF16, name="x_raw%d%d" % (b, c))
+                rows = xp[b, c * P * PACK : (c + 1) * P * PACK, :]
+                nc.sync.dma_start(out=t[:], in_=rows.rearrange("(p j) w -> p j w", j=PACK))
+                x_raw[(b, c)] = t
+            if b == 0:
+                nc.sync.dma_start(out=cb[:], in_=codebook)
+
+        neg_ones = keep.tile([P, ONES], BF16, name="neg_ones")
+        nc.vector.memset(neg_ones[:], -1.0)
+
+        steps = [("a", b, 0, 0, 0) for b in range(B)]
+        for b in range(B):
+            for c in range(PASSES):
+                if b == B - 1 and c == PASSES - 1:
+                    steps.append(("x", b, c, 0, 512))
+                    steps.append(("x", b, c, 512, 512))
+                else:
+                    steps.append(("x", b, c, 0, C))
+
+        grouped = {}
+        a_codes = {}
+        a_scales = {}
+        x_codes = {}
+        x_scales = {}
+        neg_sum = {}
+        acc = {}
+        result = {}
+
+        def do_regroup(i):
+            kind, b, c, col0, width = steps[i]
+            if kind == "a":
+                g = stage.tile([P, PASSES, K, PACK], BF16, name="ga", align_bytes=64)
+                regroup(nc.vector.tensor_copy, g[:, 0, :, :], a_raw[b][:, 0, :, :])
+                regroup(nc.scalar.copy, g[:, 1, :, :], a_raw[b][:, 1, :, :])
+                sums = ps_sum.tile([P, ONES], F32, name="sums")
+                for r in range(PASSES * PACK):
+                    nc.tensor.matmul(
+                        out=sums[:],
+                        lhsT=a_raw[b][:, r // PACK, r % PACK, :],
+                        rhs=neg_ones[:],
+                        start=(r == 0),
+                        stop=(r == PASSES * PACK - 1),
+                    )
+                neg_sum[b] = keep.tile([P, 1], F32, name="neg_sum%d" % b)
+                nc.scalar.copy(out=neg_sum[b][:], in_=sums[:, 0:1])
+            else:
+                g = stage.tile([P, width, PACK], BF16, name="gx", align_bytes=64)
+                cut = VECTOR_COLS[width]
+                src = x_raw[(b, c)]
+                regroup(nc.vector.tensor_copy, g[:, 0:cut, :], src[:, :, col0 : col0 + cut])
+                regroup(nc.scalar.copy, g[:, cut:width, :], src[:, :, col0 + cut : col0 + width])
+            grouped[i] = g
+
+        def do_multiply(i):
+            kind, b, c, col0, width = steps[i]
+            g = grouped[i]
+            if kind == "a":
+                a_codes[b] = keep.tile([P, PASSES * K], U32, name="a_codes%d" % b, align_bytes=64)
+                a_scales[b] = keep.tile([P, PASSES * K], U8, name="a_scales%d" % b, align_bytes=64)
+                nc.vector.quantize_mx(
+                    out=a_codes[b][:].bitcast(FP8X4),
+                    scales=a_scales[b][:],
+                    in_=g[:].rearrange("p c k j -> p (c k j)"),
+                )
+                return
+            if col0 == 0:
+                x_codes[(b, c)] = keep.tile([P, C], U32, name="x_codes%d%d" % (b, c), align_bytes=64)
+                x_scales[(b, c)] = keep.tile([P, C], U8, name="x_scales%d%d" % (b, c), align_bytes=64)
+            codes = x_codes[(b, c)]
+            scales = x_scales[(b, c)]
+            nc.vector.quantize_mx(
+                out=codes[:, col0 : col0 + width].bitcast(FP8X4),
+                scales=scales[:, col0 : col0 + width],
+                in_=g[:].rearrange("p w j -> p (w j)"),
+            )
+            for n0 in range(col0, col0 + width, N_TILE):
+                if c == 0:
+                    acc[(b, n0)] = ps_acc.tile([P, N_TILE], F32, name="acc")
+                nc.tensor.matmul_mx(
+                    out=acc[(b, n0)][:],
+                    lhsT=a_codes[b][:, c * K : (c + 1) * K].bitcast(FP8X4),
+                    lhsT_scale=a_scales[b][:, c * K : (c + 1) * K],
+                    rhs=codes[:, n0 : n0 + N_TILE].bitcast(FP8X4),
+                    rhs_scale=scales[:, n0 : n0 + N_TILE],
+                    start=(c == 0),
+                    stop=(c == PASSES - 1),
+                )
+
+        def do_finish(i):
+            kind, b, c, col0, width = steps[i]
+            if kind == "a" or c < PASSES - 1:
+                return
+            if col0 == 0:
+                result[b] = keep.tile([P, C], F32, name="result%d" % b)
+            for n0 in range(col0, col0 + width, N_TILE):
+                nc.vector.scalar_tensor_tensor(
+                    out=result[b][:, n0 : n0 + N_TILE],
+                    in0=cb[:, n0 : n0 + N_TILE],
+                    scalar=neg_sum[b][:, 0:1],
+                    in1=acc[(b, n0)][:],
+                    op0=mybir.AluOpType.mult,
+                    op1=mybir.AluOpType.add,
+                )
+            nc.sync.dma_start(out=out[b, :, col0 : col0 + width], in_=result[b][:, col0 : col0 + width])
+
+        for i in range(len(steps) + 2):
+            if i < len(steps):
+                do_regroup(i)
+            if 1 <= i <= len(steps):
+                do_multiply(i - 1)
+            if i >= 2:
+                do_finish(i - 2)

@@ -15,12 +15,17 @@ C = 1024
 P = 128
 PACK = 4
 PASSES = NPIX // (P * PACK)
-N_TILE = 512
 ONES = 32
 
 FLOPS = 2 * B * NPIX * K * C
 
-VECTOR_COLS = {1024: 416, 512: 208, 256: 104}
+PIECE = 512
+VECTOR_COLS = (256, 224, 192, 144)
+TAIL_PIECE = 256
+TAIL_VECTOR_COLS = (64, 64, 96, 144)
+GROUP_COLS = (512, 512, 512, 256)
+FINISH_LAG = 2
+FIRST_FINISH_LAG = 6
 
 
 def regroup(copy, dst, src):
@@ -34,78 +39,77 @@ def tile_lvc_pb_kernel(tc, assign, xp, codebook, out):
     nc = tc.nc
     with ExitStack() as ctx:
         raw = ctx.enter_context(tc.tile_pool(name="raw", bufs=1))
-        stage = ctx.enter_context(tc.tile_pool(name="stage", bufs=3))
+        stage = ctx.enter_context(tc.tile_pool(name="stage", bufs=4))
         keep = ctx.enter_context(tc.tile_pool(name="keep", bufs=1))
-        ps_acc = ctx.enter_context(tc.psum_pool(name="ps_acc", bufs=6))
-        ps_sum = ctx.enter_context(tc.psum_pool(name="ps_sum", bufs=2))
+        ps_acc = ctx.enter_context(tc.psum_pool(name="ps_acc", bufs=7))
+        ps_sum = ctx.enter_context(tc.psum_pool(name="ps_sum", bufs=1))
+        ctx.enter_context(tc.manual_schedule())
 
         a_raw = []
+        x_raw = {}
+        cb = raw.tile([P, C], BF16, name="cb")
         for b in range(B):
+            if b == 2:
+                nc.sync.dma_start(out=cb[:], in_=codebook)
             t = raw.tile([P, PASSES, PACK, K], BF16, name="a_raw%d" % b)
             nc.sync.dma_start(
                 out=t[:],
                 in_=assign[b, :, :].rearrange("(c p j) k -> p c j k", c=PASSES, p=P, j=PACK),
             )
             a_raw.append(t)
-        x_raw = {}
-        cb = raw.tile([P, C], BF16, name="cb")
-        for b in range(B):
             for c in range(PASSES):
                 t = raw.tile([P, PACK, C], BF16, name="x_raw%d%d" % (b, c))
                 rows = xp[b, c * P * PACK : (c + 1) * P * PACK, :]
                 nc.sync.dma_start(out=t[:], in_=rows.rearrange("(p j) w -> p j w", j=PACK))
                 x_raw[(b, c)] = t
-            if b == 0:
-                nc.sync.dma_start(out=cb[:], in_=codebook)
 
         neg_ones = keep.tile([P, ONES], BF16, name="neg_ones")
         nc.vector.memset(neg_ones[:], -1.0)
+        sums = ps_sum.tile([P, B, ONES], F32, name="sums")
+        neg_sum = keep.tile([P, B], F32, name="neg_sum")
 
-        steps = [("a", b, 0, 0, 0) for b in range(B)]
+        steps = []
         for b in range(B):
+            steps.append(("a", b, 0, 0, 0, 0))
             for c in range(PASSES):
                 if b == B - 1 and c == PASSES - 1:
-                    steps.append(("x", b, c, 0, 512))
-                    steps.append(("x", b, c, 512, 512))
+                    for q in range(C // TAIL_PIECE):
+                        steps.append(("x", b, c, q * TAIL_PIECE, TAIL_PIECE, TAIL_VECTOR_COLS[q]))
                 else:
-                    steps.append(("x", b, c, 0, C))
+                    for q in range(C // PIECE):
+                        steps.append(("x", b, c, q * PIECE, PIECE, VECTOR_COLS[b]))
 
         grouped = {}
         a_codes = {}
         a_scales = {}
         x_codes = {}
         x_scales = {}
-        neg_sum = {}
         acc = {}
         result = {}
 
         def do_regroup(i):
-            kind, b, c, col0, width = steps[i]
+            kind, b, c, col0, width, cut = steps[i]
             if kind == "a":
                 g = stage.tile([P, PASSES, K, PACK], BF16, name="ga", align_bytes=64)
                 regroup(nc.vector.tensor_copy, g[:, 0, :, :], a_raw[b][:, 0, :, :])
                 regroup(nc.scalar.copy, g[:, 1, :, :], a_raw[b][:, 1, :, :])
-                sums = ps_sum.tile([P, ONES], F32, name="sums")
                 for r in range(PASSES * PACK):
                     nc.tensor.matmul(
-                        out=sums[:],
+                        out=sums[:, b, :],
                         lhsT=a_raw[b][:, r // PACK, r % PACK, :],
                         rhs=neg_ones[:],
                         start=(r == 0),
                         stop=(r == PASSES * PACK - 1),
                     )
-                neg_sum[b] = keep.tile([P, 1], F32, name="neg_sum%d" % b)
-                nc.scalar.copy(out=neg_sum[b][:], in_=sums[:, 0:1])
             else:
                 g = stage.tile([P, width, PACK], BF16, name="gx", align_bytes=64)
-                cut = VECTOR_COLS[width]
                 src = x_raw[(b, c)]
                 regroup(nc.vector.tensor_copy, g[:, 0:cut, :], src[:, :, col0 : col0 + cut])
                 regroup(nc.scalar.copy, g[:, cut:width, :], src[:, :, col0 + cut : col0 + width])
             grouped[i] = g
 
         def do_multiply(i):
-            kind, b, c, col0, width = steps[i]
+            kind, b, c, col0, width, cut = steps[i]
             g = grouped[i]
             if kind == "a":
                 a_codes[b] = keep.tile([P, PASSES * K], U32, name="a_codes%d" % b, align_bytes=64)
@@ -115,6 +119,7 @@ def tile_lvc_pb_kernel(tc, assign, xp, codebook, out):
                     scales=a_scales[b][:],
                     in_=g[:].rearrange("p c k j -> p (c k j)"),
                 )
+                nc.vector.tensor_copy(out=neg_sum[:, b : b + 1], in_=sums[:, b, 0:1])
                 return
             if col0 == 0:
                 x_codes[(b, c)] = keep.tile([P, C], U32, name="x_codes%d%d" % (b, c), align_bytes=64)
@@ -126,40 +131,45 @@ def tile_lvc_pb_kernel(tc, assign, xp, codebook, out):
                 scales=scales[:, col0 : col0 + width],
                 in_=g[:].rearrange("p w j -> p (w j)"),
             )
-            for n0 in range(col0, col0 + width, N_TILE):
+            ns = GROUP_COLS[b]
+            for n0 in range(col0, col0 + width, ns):
                 if c == 0:
-                    acc[(b, n0)] = ps_acc.tile([P, N_TILE], F32, name="acc")
+                    acc[(b, n0)] = ps_acc.tile([P, ns], F32, name="acc")
                 nc.tensor.matmul_mx(
                     out=acc[(b, n0)][:],
                     lhsT=a_codes[b][:, c * K : (c + 1) * K].bitcast(FP8X4),
                     lhsT_scale=a_scales[b][:, c * K : (c + 1) * K],
-                    rhs=codes[:, n0 : n0 + N_TILE].bitcast(FP8X4),
-                    rhs_scale=scales[:, n0 : n0 + N_TILE],
+                    rhs=codes[:, n0 : n0 + ns].bitcast(FP8X4),
+                    rhs_scale=scales[:, n0 : n0 + ns],
                     start=(c == 0),
                     stop=(c == PASSES - 1),
                 )
 
         def do_finish(i):
-            kind, b, c, col0, width = steps[i]
-            if kind == "a" or c < PASSES - 1:
-                return
+            kind, b, c, col0, width, cut = steps[i]
             if col0 == 0:
                 result[b] = keep.tile([P, C], F32, name="result%d" % b)
-            for n0 in range(col0, col0 + width, N_TILE):
+            ns = GROUP_COLS[b]
+            for n0 in range(col0, col0 + width, ns):
                 nc.vector.scalar_tensor_tensor(
-                    out=result[b][:, n0 : n0 + N_TILE],
-                    in0=cb[:, n0 : n0 + N_TILE],
-                    scalar=neg_sum[b][:, 0:1],
+                    out=result[b][:, n0 : n0 + ns],
+                    in0=cb[:, n0 : n0 + ns],
+                    scalar=neg_sum[:, b : b + 1],
                     in1=acc[(b, n0)][:],
                     op0=mybir.AluOpType.mult,
                     op1=mybir.AluOpType.add,
                 )
             nc.sync.dma_start(out=out[b, :, col0 : col0 + width], in_=result[b][:, col0 : col0 + width])
 
-        for i in range(len(steps) + 2):
+        finish_at = {}
+        for i in range(len(steps)):
+            if steps[i][0] == "x" and steps[i][2] == PASSES - 1:
+                lag = FIRST_FINISH_LAG if steps[i][1] == 0 else FINISH_LAG
+                finish_at[i + lag] = finish_at.get(i + lag, []) + [i]
+        for i in range(len(steps) + FINISH_LAG + 1):
             if i < len(steps):
                 do_regroup(i)
             if 1 <= i <= len(steps):
                 do_multiply(i - 1)
-            if i >= 2:
-                do_finish(i - 2)
+            for j in finish_at.get(i, []):
+                do_finish(j)

@@ -20,12 +20,15 @@ ONES = 32
 FLOPS = 2 * B * NPIX * K * C
 
 PIECE = 512
-VECTOR_COLS = (256, 224, 192, 144)
-TAIL_PIECE = 256
-TAIL_VECTOR_COLS = (64, 64, 96, 144)
-GROUP_COLS = (512, 512, 512, 256)
-FINISH_LAG = 2
-FIRST_FINISH_LAG = 6
+VECTOR_COLS = (256, 224, 192, 176)
+TAIL_PIECES = ((256, 32), (256, 128), (256, 128), (128, 0), (128, 32))
+BANK = 512
+FINISH_LAG = 3
+FIRST_FINISH_LAG = 3
+STAGE_BUFS = 4
+Q_LAG = 1
+ORDER = (("x", 0, 0), ("x", 0, 1), ("a", 0), ("x", 1, 0), ("x", 1, 1), ("a", 1), ("cb",), ("x", 2, 0), ("x", 2, 1), ("a", 2), ("a", 3), ("x", 3, 0), ("x", 3, 1))
+LOAD_COLS = {}
 
 
 def regroup(copy, dst, src):
@@ -39,29 +42,34 @@ def tile_lvc_pb_kernel(tc, assign, xp, codebook, out):
     nc = tc.nc
     with ExitStack() as ctx:
         raw = ctx.enter_context(tc.tile_pool(name="raw", bufs=1))
-        stage = ctx.enter_context(tc.tile_pool(name="stage", bufs=4))
+        stage = ctx.enter_context(tc.tile_pool(name="stage", bufs=STAGE_BUFS))
         keep = ctx.enter_context(tc.tile_pool(name="keep", bufs=1))
         ps_acc = ctx.enter_context(tc.psum_pool(name="ps_acc", bufs=7))
         ps_sum = ctx.enter_context(tc.psum_pool(name="ps_sum", bufs=1))
         ctx.enter_context(tc.manual_schedule())
 
-        a_raw = []
+        a_raw = {}
         x_raw = {}
         cb = raw.tile([P, C], BF16, name="cb")
-        for b in range(B):
-            if b == 2:
+        for item in ORDER:
+            if item[0] == "cb":
                 nc.sync.dma_start(out=cb[:], in_=codebook)
-            t = raw.tile([P, PASSES, PACK, K], BF16, name="a_raw%d" % b)
-            nc.sync.dma_start(
-                out=t[:],
-                in_=assign[b, :, :].rearrange("(c p j) k -> p c j k", c=PASSES, p=P, j=PACK),
-            )
-            a_raw.append(t)
-            for c in range(PASSES):
-                t = raw.tile([P, PACK, C], BF16, name="x_raw%d%d" % (b, c))
-                rows = xp[b, c * P * PACK : (c + 1) * P * PACK, :]
-                nc.sync.dma_start(out=t[:], in_=rows.rearrange("(p j) w -> p j w", j=PACK))
-                x_raw[(b, c)] = t
+            elif item[0] == "a":
+                b = item[1]
+                t = raw.tile([P, PASSES, PACK, K], BF16, name="a_raw%d" % b)
+                nc.sync.dma_start(
+                    out=t[:],
+                    in_=assign[b, :, :].rearrange("(c p j) k -> p c j k", c=PASSES, p=P, j=PACK),
+                )
+                a_raw[b] = t
+            else:
+                b, c = item[1], item[2]
+                lw = LOAD_COLS.get((b, c), C)
+                for w0 in range(0, C, lw):
+                    t = raw.tile([P, PACK, lw], BF16, name="x_raw%d%d_%d" % (b, c, w0))
+                    rows = xp[b, c * P * PACK : (c + 1) * P * PACK, w0 : w0 + lw]
+                    nc.sync.dma_start(out=t[:], in_=rows.rearrange("(p j) w -> p j w", j=PACK))
+                    x_raw[(b, c, w0)] = t
 
         neg_ones = keep.tile([P, ONES], BF16, name="neg_ones")
         nc.vector.memset(neg_ones[:], -1.0)
@@ -69,15 +77,27 @@ def tile_lvc_pb_kernel(tc, assign, xp, codebook, out):
         neg_sum = keep.tile([P, B], F32, name="neg_sum")
 
         steps = []
-        for b in range(B):
-            steps.append(("a", b, 0, 0, 0, 0))
-            for c in range(PASSES):
+        for item in ORDER:
+            if item[0] == "a":
+                steps.append(("a", item[1], 0, 0, 0, 0))
+            elif item[0] == "x":
+                b, c = item[1], item[2]
                 if b == B - 1 and c == PASSES - 1:
-                    for q in range(C // TAIL_PIECE):
-                        steps.append(("x", b, c, q * TAIL_PIECE, TAIL_PIECE, TAIL_VECTOR_COLS[q]))
+                    col0 = 0
+                    for width, cut in TAIL_PIECES:
+                        steps.append(("x", b, c, col0, width, cut))
+                        col0 += width
                 else:
                     for q in range(C // PIECE):
                         steps.append(("x", b, c, q * PIECE, PIECE, VECTOR_COLS[b]))
+
+        def groups(b):
+            if b < B - 1:
+                return [(n0, BANK) for n0 in range(0, C, BANK)]
+            found = []
+            for width, cut in TAIL_PIECES:
+                found.append((sum(w for n, w in found), width))
+            return found
 
         grouped = {}
         a_codes = {}
@@ -86,6 +106,7 @@ def tile_lvc_pb_kernel(tc, assign, xp, codebook, out):
         x_scales = {}
         acc = {}
         result = {}
+        waiting = []
 
         def do_regroup(i):
             kind, b, c, col0, width, cut = steps[i]
@@ -103,10 +124,27 @@ def tile_lvc_pb_kernel(tc, assign, xp, codebook, out):
                     )
             else:
                 g = stage.tile([P, width, PACK], BF16, name="gx", align_bytes=64)
-                src = x_raw[(b, c)]
-                regroup(nc.vector.tensor_copy, g[:, 0:cut, :], src[:, :, col0 : col0 + cut])
-                regroup(nc.scalar.copy, g[:, cut:width, :], src[:, :, col0 + cut : col0 + width])
+                lw = LOAD_COLS.get((b, c), C)
+                src = x_raw[(b, c, col0 - col0 % lw)]
+                l0 = col0 % lw
+                if cut > 0:
+                    regroup(nc.vector.tensor_copy, g[:, 0:cut, :], src[:, :, l0 : l0 + cut])
+                if cut < width:
+                    regroup(nc.scalar.copy, g[:, cut:width, :], src[:, :, l0 + cut : l0 + width])
             grouped[i] = g
+
+        def product(b, c, n0, ns):
+            if c == 0:
+                acc[(b, n0)] = ps_acc.tile([P, ns], F32, name="acc")
+            nc.tensor.matmul_mx(
+                out=acc[(b, n0)][:],
+                lhsT=a_codes[b][:, c * K : (c + 1) * K].bitcast(FP8X4),
+                lhsT_scale=a_scales[b][:, c * K : (c + 1) * K],
+                rhs=x_codes[(b, c)][:, n0 : n0 + ns].bitcast(FP8X4),
+                rhs_scale=x_scales[(b, c)][:, n0 : n0 + ns],
+                start=(c == 0),
+                stop=(c == PASSES - 1),
+            )
 
         def do_multiply(i):
             kind, b, c, col0, width, cut = steps[i]
@@ -120,37 +158,29 @@ def tile_lvc_pb_kernel(tc, assign, xp, codebook, out):
                     in_=g[:].rearrange("p c k j -> p (c k j)"),
                 )
                 nc.vector.tensor_copy(out=neg_sum[:, b : b + 1], in_=sums[:, b, 0:1])
+                for late in waiting:
+                    product(*late)
+                waiting.clear()
                 return
             if col0 == 0:
                 x_codes[(b, c)] = keep.tile([P, C], U32, name="x_codes%d%d" % (b, c), align_bytes=64)
                 x_scales[(b, c)] = keep.tile([P, C], U8, name="x_scales%d%d" % (b, c), align_bytes=64)
-            codes = x_codes[(b, c)]
-            scales = x_scales[(b, c)]
             nc.vector.quantize_mx(
-                out=codes[:, col0 : col0 + width].bitcast(FP8X4),
-                scales=scales[:, col0 : col0 + width],
+                out=x_codes[(b, c)][:, col0 : col0 + width].bitcast(FP8X4),
+                scales=x_scales[(b, c)][:, col0 : col0 + width],
                 in_=g[:].rearrange("p w j -> p (w j)"),
             )
-            ns = GROUP_COLS[b]
-            for n0 in range(col0, col0 + width, ns):
-                if c == 0:
-                    acc[(b, n0)] = ps_acc.tile([P, ns], F32, name="acc")
-                nc.tensor.matmul_mx(
-                    out=acc[(b, n0)][:],
-                    lhsT=a_codes[b][:, c * K : (c + 1) * K].bitcast(FP8X4),
-                    lhsT_scale=a_scales[b][:, c * K : (c + 1) * K],
-                    rhs=codes[:, n0 : n0 + ns].bitcast(FP8X4),
-                    rhs_scale=scales[:, n0 : n0 + ns],
-                    start=(c == 0),
-                    stop=(c == PASSES - 1),
-                )
+            for n0, ns in [g for g in groups(b) if col0 < g[0] + g[1] <= col0 + width]:
+                if b in a_codes:
+                    product(b, c, n0, ns)
+                else:
+                    waiting.append((b, c, n0, ns))
 
         def do_finish(i):
             kind, b, c, col0, width, cut = steps[i]
             if col0 == 0:
                 result[b] = keep.tile([P, C], F32, name="result%d" % b)
-            ns = GROUP_COLS[b]
-            for n0 in range(col0, col0 + width, ns):
+            for n0, ns in [g for g in groups(b) if col0 < g[0] + g[1] <= col0 + width]:
                 nc.vector.scalar_tensor_tensor(
                     out=result[b][:, n0 : n0 + ns],
                     in0=cb[:, n0 : n0 + ns],
@@ -165,11 +195,12 @@ def tile_lvc_pb_kernel(tc, assign, xp, codebook, out):
         for i in range(len(steps)):
             if steps[i][0] == "x" and steps[i][2] == PASSES - 1:
                 lag = FIRST_FINISH_LAG if steps[i][1] == 0 else FINISH_LAG
-                finish_at[i + lag] = finish_at.get(i + lag, []) + [i]
-        for i in range(len(steps) + FINISH_LAG + 1):
+                at = max(i, steps.index(("a", steps[i][1], 0, 0, 0, 0))) + lag
+                finish_at[at] = finish_at.get(at, []) + [i]
+        for i in range(len(steps) + FINISH_LAG + Q_LAG):
             if i < len(steps):
                 do_regroup(i)
-            if 1 <= i <= len(steps):
-                do_multiply(i - 1)
-            for j in finish_at.get(i, []):
+            if 0 <= i - Q_LAG < len(steps):
+                do_multiply(i - Q_LAG)
+            for j in finish_at.get(i - Q_LAG + 1, []):
                 do_finish(j)

@@ -25,6 +25,7 @@ TAIL_PIECES = ((256, 32), (256, 128), (256, 128), (128, 0), (128, 32))
 BANK = 512
 FINISH_LAG = 3
 FIRST_FINISH_LAG = 3
+LAST_FINISH_LAG = 4
 STAGE_BUFS = 4
 Q_LAG = 1
 ORDER = (("x", 0, 0), ("x", 0, 1), ("a", 0), ("x", 1, 0), ("x", 1, 1), ("a", 1), ("cb",), ("x", 2, 0), ("x", 2, 1), ("a", 2), ("a", 3), ("x", 3, 0), ("x", 3, 1))
@@ -194,10 +195,10 @@ def tile_lvc_pb_kernel(tc, assign, xp, codebook, out):
         finish_at = {}
         for i in range(len(steps)):
             if steps[i][0] == "x" and steps[i][2] == PASSES - 1:
-                lag = FIRST_FINISH_LAG if steps[i][1] == 0 else FINISH_LAG
+                lag = FIRST_FINISH_LAG if steps[i][1] == 0 else (LAST_FINISH_LAG if steps[i][1] == B - 1 else FINISH_LAG)
                 at = max(i, steps.index(("a", steps[i][1], 0, 0, 0, 0))) + lag
                 finish_at[at] = finish_at.get(at, []) + [i]
-        for i in range(len(steps) + FINISH_LAG + Q_LAG):
+        for i in range(len(steps) + LAST_FINISH_LAG + Q_LAG):
             if i < len(steps):
                 do_regroup(i)
             if 0 <= i - Q_LAG < len(steps):

@@ -20,14 +20,17 @@ ONES = 32
 FLOPS = 2 * B * NPIX * K * C
 
 PIECE = 512
-VECTOR_COLS = (256, 224, 192, 176)
-TAIL_PIECES = ((256, 32), (256, 128), (256, 128), (128, 0), (128, 32))
+VECTOR_COLS = (288, 256, 240, 240)
+TAIL_PIECES = ((256, 128), (256, 160), (256, 128), (128, 0), (128, 32))
 BANK = 512
 FINISH_LAG = 3
-FIRST_FINISH_LAG = 3
+FIRST_FINISH_LAG = 4
 LAST_FINISH_LAG = 4
 STAGE_BUFS = 4
 Q_LAG = 1
+ONE_COPY = True
+A_ON_SCALAR = True
+SUM_ON_SCALAR = True
 ORDER = (("x", 0, 0), ("x", 0, 1), ("a", 0), ("x", 1, 0), ("x", 1, 1), ("a", 1), ("cb",), ("x", 2, 0), ("x", 2, 1), ("a", 2), ("a", 3), ("x", 3, 0), ("x", 3, 1))
 LOAD_COLS = {}
 
@@ -90,7 +93,10 @@ def tile_lvc_pb_kernel(tc, assign, xp, codebook, out):
                         col0 += width
                 else:
                     for q in range(C // PIECE):
-                        steps.append(("x", b, c, q * PIECE, PIECE, VECTOR_COLS[b]))
+                        if ONE_COPY:
+                            steps.append(("x", b, c, q * PIECE, PIECE, min(PIECE, 2 * VECTOR_COLS[b]) if q == 0 else max(0, 2 * VECTOR_COLS[b] - PIECE)))
+                        else:
+                            steps.append(("x", b, c, q * PIECE, PIECE, VECTOR_COLS[b]))
 
         def groups(b):
             if b < B - 1:
@@ -113,7 +119,7 @@ def tile_lvc_pb_kernel(tc, assign, xp, codebook, out):
             kind, b, c, col0, width, cut = steps[i]
             if kind == "a":
                 g = stage.tile([P, PASSES, K, PACK], BF16, name="ga", align_bytes=64)
-                regroup(nc.vector.tensor_copy, g[:, 0, :, :], a_raw[b][:, 0, :, :])
+                regroup(nc.scalar.copy if A_ON_SCALAR else nc.vector.tensor_copy, g[:, 0, :, :], a_raw[b][:, 0, :, :])
                 regroup(nc.scalar.copy, g[:, 1, :, :], a_raw[b][:, 1, :, :])
                 for r in range(PASSES * PACK):
                     nc.tensor.matmul(
@@ -123,6 +129,8 @@ def tile_lvc_pb_kernel(tc, assign, xp, codebook, out):
                         start=(r == 0),
                         stop=(r == PASSES * PACK - 1),
                     )
+                if SUM_ON_SCALAR:
+                    nc.scalar.copy(out=neg_sum[:, b : b + 1], in_=sums[:, b, 0:1])
             else:
                 g = stage.tile([P, width, PACK], BF16, name="gx", align_bytes=64)
                 lw = LOAD_COLS.get((b, c), C)
@@ -158,7 +166,8 @@ def tile_lvc_pb_kernel(tc, assign, xp, codebook, out):
                     scales=a_scales[b][:],
                     in_=g[:].rearrange("p c k j -> p (c k j)"),
                 )
-                nc.vector.tensor_copy(out=neg_sum[:, b : b + 1], in_=sums[:, b, 0:1])
+                if not SUM_ON_SCALAR:
+                    nc.vector.tensor_copy(out=neg_sum[:, b : b + 1], in_=sums[:, b, 0:1])
                 for late in waiting:
                     product(*late)
                 waiting.clear()

@@ -19,6 +19,7 @@ ONES = 32
 
 FLOPS = 2 * B * NPIX * K * C
 
+RUN = 8
 PIECE = 512
 VECTOR_COLS = (288, 256, 240, 240)
 TAIL_PIECES = ((256, 128), (256, 160), (256, 128), (128, 0), (128, 32))
@@ -37,8 +38,8 @@ LOAD_COLS = {}
 
 def regroup(copy, dst, src):
     copy(
-        out=dst.rearrange("p (c i) j -> p c j i", i=4),
-        in_=src.rearrange("p j (c i) -> p c j i", i=4),
+        out=dst.rearrange("p (c i) j -> p c j i", i=RUN),
+        in_=src.rearrange("p j (c i) -> p c j i", i=RUN),
     )
 
 

@@ -21,14 +21,16 @@ FLOPS = 2 * B * NPIX * K * C
 
 RUN = 8
 PIECE = 512
-VECTOR_COLS = (288, 256, 240, 240)
-TAIL_PIECES = ((256, 128), (256, 160), (256, 128), (128, 0), (128, 32))
+VECTOR_COLS = (256, 240, 224, 208)
+TAIL_PIECES = ((256, 64), (256, 160), (256, 96), (128, 0), (128, 0))
 BANK = 512
 FINISH_LAG = 3
 FIRST_FINISH_LAG = 4
-LAST_FINISH_LAG = 4
-STAGE_BUFS = 4
+LAST_FINISH_LAG = 3
+STAGE_BUFS = 6
 Q_LAG = 1
+GPSIMD_COLS = 128
+GPSIMD_CHUNKS = ((1, 1), (2, 1), (3, 0))
 ONE_COPY = True
 A_ON_SCALAR = True
 SUM_ON_SCALAR = True
@@ -94,7 +96,11 @@ def tile_lvc_pb_kernel(tc, assign, xp, codebook, out):
                         col0 += width
                 else:
                     for q in range(C // PIECE):
-                        if ONE_COPY:
+                        if q == 1 and (b, c) in GPSIMD_CHUNKS:
+                            steps.append(("x", b, c, PIECE, PIECE // 2, 0))
+                            steps.append(("x", b, c, PIECE + PIECE // 2, PIECE // 2 - GPSIMD_COLS, 0))
+                            steps.append(("g", b, c, C - GPSIMD_COLS, GPSIMD_COLS, 0))
+                        elif ONE_COPY:
                             steps.append(("x", b, c, q * PIECE, PIECE, min(PIECE, 2 * VECTOR_COLS[b]) if q == 0 else max(0, 2 * VECTOR_COLS[b] - PIECE)))
                         else:
                             steps.append(("x", b, c, q * PIECE, PIECE, VECTOR_COLS[b]))
@@ -118,6 +124,8 @@ def tile_lvc_pb_kernel(tc, assign, xp, codebook, out):
 
         def do_regroup(i):
             kind, b, c, col0, width, cut = steps[i]
+            if kind == "g":
+                return
             if kind == "a":
                 g = stage.tile([P, PASSES, K, PACK], BF16, name="ga", align_bytes=64)
                 regroup(nc.scalar.copy if A_ON_SCALAR else nc.vector.tensor_copy, g[:, 0, :, :], a_raw[b][:, 0, :, :])
@@ -141,6 +149,19 @@ def tile_lvc_pb_kernel(tc, assign, xp, codebook, out):
                     regroup(nc.vector.tensor_copy, g[:, 0:cut, :], src[:, :, l0 : l0 + cut])
                 if cut < width:
                     regroup(nc.scalar.copy, g[:, cut:width, :], src[:, :, l0 + cut : l0 + width])
+            grouped[i] = g
+
+        def gpsimd_regroup(i, old):
+            kind, b, c, col0, width, cut = steps[i]
+            g = old[:, 0:width, :]
+            nc.gpsimd.tensor_scalar(
+                out=g,
+                in0=x_raw[(b, c, 0)][:, :, col0 : col0 + width].rearrange("p j w -> p w j"),
+                scalar1=1.0,
+                scalar2=0.0,
+                op0=mybir.AluOpType.mult,
+                op1=mybir.AluOpType.add,
+            )
             grouped[i] = g
 
         def product(b, c, n0, ns):
@@ -179,7 +200,7 @@ def tile_lvc_pb_kernel(tc, assign, xp, codebook, out):
             nc.vector.quantize_mx(
                 out=x_codes[(b, c)][:, col0 : col0 + width].bitcast(FP8X4),
                 scales=x_scales[(b, c)][:, col0 : col0 + width],
-                in_=g[:].rearrange("p w j -> p (w j)"),
+                in_=g.rearrange("p w j -> p (w j)") if kind == "g" else g[:].rearrange("p w j -> p (w j)"),
             )
             for n0, ns in [g for g in groups(b) if col0 < g[0] + g[1] <= col0 + width]:
                 if b in a_codes:
@@ -200,11 +221,11 @@ def tile_lvc_pb_kernel(tc, assign, xp, codebook, out):
                     op0=mybir.AluOpType.mult,
                     op1=mybir.AluOpType.add,
                 )
-            nc.sync.dma_start(out=out[b, :, col0 : col0 + width], in_=result[b][:, col0 : col0 + width])
+                nc.sync.dma_start(out=out[b, :, n0 : n0 + ns], in_=result[b][:, n0 : n0 + ns])
 
         finish_at = {}
         for i in range(len(steps)):
-            if steps[i][0] == "x" and steps[i][2] == PASSES - 1:
+            if steps[i][0] in ("x", "g") and steps[i][2] == PASSES - 1:
                 lag = FIRST_FINISH_LAG if steps[i][1] == 0 else (LAST_FINISH_LAG if steps[i][1] == B - 1 else FINISH_LAG)
                 at = max(i, steps.index(("a", steps[i][1], 0, 0, 0, 0))) + lag
                 finish_at[at] = finish_at.get(at, []) + [i]
@@ -213,5 +234,10 @@ def tile_lvc_pb_kernel(tc, assign, xp, codebook, out):
                 do_regroup(i)
             if 0 <= i - Q_LAG < len(steps):
                 do_multiply(i - Q_LAG)
-            for j in finish_at.get(i - Q_LAG + 1, []):
+            due = finish_at.get(i - Q_LAG + 1, [])
+            if due and steps[due[0]][1] < B - 1:
+                later = [s for s in range(i, len(steps)) if steps[s][0] == "g"]
+                if later and GPSIMD_COLS:
+                    gpsimd_regroup(later[0], grouped[i - Q_LAG])
+            for j in due:
                 do_finish(j)

@@ -1,6 +1,7 @@
 from contextlib import ExitStack
 
 import concourse.mybir as mybir
+from concourse.masks import make_identity
 
 FP8X4 = mybir.dt.float8_e4m3fn_x4
 BF16 = mybir.dt.bfloat16
@@ -15,14 +16,16 @@ C = 1024
 P = 128
 PACK = 4
 PASSES = NPIX // (P * PACK)
-ONES = 32
+ONES = 2
 
 FLOPS = 2 * B * NPIX * K * C
 
 RUN = 8
 PIECE = 512
 VECTOR_COLS = (256, 240, 224, 208)
-TAIL_PIECES = ((256, 64), (256, 160), (256, 96), (128, 0), (128, 0))
+TAIL_PIECES = ((256, 64), (256, 160), (256, -1), (128, 0), (128, 0))
+PIECES = {(0, 0): ((512, 512), (512, 0)), (0, 1): ((512, 512), (512, 0)), (1, 0): ((512, 480), (512, 0)), (1, 1): ((512, 480), (256, 0), (128, 0)), (2, 0): ((512, 448), (512, 0)), (2, 1): ((512, 448), (256, 0), (128, 0)), (3, 0): ((512, 416), (256, 0), (128, 0))}
+G_PIECES = ((512, 512), (256, 0), (128, 0))
 BANK = 512
 FINISH_LAG = 3
 FIRST_FINISH_LAG = 4
@@ -33,6 +36,9 @@ GPSIMD_COLS = 128
 GPSIMD_CHUNKS = ((1, 1), (2, 1), (3, 0))
 ONE_COPY = True
 A_ON_SCALAR = True
+ACC_BUFS = 6
+R_BUFS = 1
+R_ISSUE = ((("x", 3, 0, 512), ((3, 1, 512, 256),)),)
 SUM_ON_SCALAR = True
 ORDER = (("x", 0, 0), ("x", 0, 1), ("a", 0), ("x", 1, 0), ("x", 1, 1), ("a", 1), ("cb",), ("x", 2, 0), ("x", 2, 1), ("a", 2), ("a", 3), ("x", 3, 0), ("x", 3, 1))
 LOAD_COLS = {}
@@ -51,8 +57,9 @@ def tile_lvc_pb_kernel(tc, assign, xp, codebook, out):
         raw = ctx.enter_context(tc.tile_pool(name="raw", bufs=1))
         stage = ctx.enter_context(tc.tile_pool(name="stage", bufs=STAGE_BUFS))
         keep = ctx.enter_context(tc.tile_pool(name="keep", bufs=1))
-        ps_acc = ctx.enter_context(tc.psum_pool(name="ps_acc", bufs=7))
+        ps_acc = ctx.enter_context(tc.psum_pool(name="ps_acc", bufs=ACC_BUFS))
         ps_sum = ctx.enter_context(tc.psum_pool(name="ps_sum", bufs=1))
+        ps_r = ctx.enter_context(tc.psum_pool(name="ps_r", bufs=R_BUFS))
         ctx.enter_context(tc.manual_schedule())
 
         a_raw = {}
@@ -78,6 +85,8 @@ def tile_lvc_pb_kernel(tc, assign, xp, codebook, out):
                     nc.sync.dma_start(out=t[:], in_=rows.rearrange("(p j) w -> p j w", j=PACK))
                     x_raw[(b, c, w0)] = t
 
+        ident = keep.tile([P, P], BF16, name="ident")
+        make_identity(nc, ident[:])
         neg_ones = keep.tile([P, ONES], BF16, name="neg_ones")
         nc.vector.memset(neg_ones[:], -1.0)
         sums = ps_sum.tile([P, B, ONES], F32, name="sums")
@@ -92,18 +101,15 @@ def tile_lvc_pb_kernel(tc, assign, xp, codebook, out):
                 if b == B - 1 and c == PASSES - 1:
                     col0 = 0
                     for width, cut in TAIL_PIECES:
-                        steps.append(("x", b, c, col0, width, cut))
+                        steps.append(("x" if cut >= 0 else "r", b, c, col0, width, max(cut, 0)))
                         col0 += width
                 else:
-                    for q in range(C // PIECE):
-                        if q == 1 and (b, c) in GPSIMD_CHUNKS:
-                            steps.append(("x", b, c, PIECE, PIECE // 2, 0))
-                            steps.append(("x", b, c, PIECE + PIECE // 2, PIECE // 2 - GPSIMD_COLS, 0))
-                            steps.append(("g", b, c, C - GPSIMD_COLS, GPSIMD_COLS, 0))
-                        elif ONE_COPY:
-                            steps.append(("x", b, c, q * PIECE, PIECE, min(PIECE, 2 * VECTOR_COLS[b]) if q == 0 else max(0, 2 * VECTOR_COLS[b] - PIECE)))
-                        else:
-                            steps.append(("x", b, c, q * PIECE, PIECE, VECTOR_COLS[b]))
+                    col0 = 0
+                    for width, cut in PIECES[(b, c)]:
+                        steps.append(("x" if cut >= 0 else "r", b, c, col0, width, max(cut, 0)))
+                        col0 += width
+                    if (b, c) in GPSIMD_CHUNKS:
+                        steps.append(("g", b, c, C - GPSIMD_COLS, GPSIMD_COLS, 0))
 
         def groups(b):
             if b < B - 1:
@@ -122,9 +128,33 @@ def tile_lvc_pb_kernel(tc, assign, xp, codebook, out):
         result = {}
         waiting = []
 
+        r_bank = {}
+
+        def tensor_regroup(b, c, col0, width):
+            bank = ps_r.tile([P, width, PACK], BF16, name="rg")
+            for w0 in range(0, width, P):
+                nc.tensor.matmul(
+                    out=bank[:, w0 : w0 + P, :],
+                    lhsT=ident[:],
+                    rhs=x_raw[(b, c, 0)][:, :, col0 + w0 : col0 + w0 + P].rearrange("p j w -> p w j"),
+                    start=True,
+                    stop=True,
+                )
+            r_bank[(b, c, col0)] = bank
+
         def do_regroup(i):
             kind, b, c, col0, width, cut = steps[i]
+            for key, banks in R_ISSUE:
+                if steps[i][:4] == key:
+                    for bank in banks:
+                        tensor_regroup(*bank)
             if kind == "g":
+                return
+            if kind == "r":
+                g = stage.tile([P, width, PACK], BF16, name="gx", align_bytes=64)
+                b0 = max(k[2] for k in r_bank if k[:2] == (b, c) and k[2] <= col0)
+                nc.scalar.copy(out=g[:], in_=r_bank[(b, c, b0)][:, col0 - b0 : col0 - b0 + width, :])
+                grouped[i] = g
                 return
             if kind == "a":
                 g = stage.tile([P, PASSES, K, PACK], BF16, name="ga", align_bytes=64)
@@ -225,9 +255,10 @@ def tile_lvc_pb_kernel(tc, assign, xp, codebook, out):
 
         finish_at = {}
         for i in range(len(steps)):
-            if steps[i][0] in ("x", "g") and steps[i][2] == PASSES - 1:
+            if steps[i][0] in ("x", "g", "r") and steps[i][2] == PASSES - 1:
                 lag = FIRST_FINISH_LAG if steps[i][1] == 0 else (LAST_FINISH_LAG if steps[i][1] == B - 1 else FINISH_LAG)
-                at = max(i, steps.index(("a", steps[i][1], 0, 0, 0, 0))) + lag
+                last = max(s for s in range(len(steps)) if steps[s][1] == steps[i][1] and steps[s][0] != "a")
+                at = max(i if steps[i][1] == B - 1 else last, steps.index(("a", steps[i][1], 0, 0, 0, 0))) + lag
                 finish_at[at] = finish_at.get(at, []) + [i]
         for i in range(len(steps) + LAST_FINISH_LAG + Q_LAG):
             if i < len(steps):

@@ -23,7 +23,7 @@ FLOPS = 2 * B * NPIX * K * C
 RUN = 8
 PIECE = 512
 VECTOR_COLS = (256, 240, 224, 208)
-TAIL_PIECES = ((256, 64), (256, 160), (256, -1), (128, 0), (128, 0))
+TAIL_PIECES = ((256, 0), (256, 160), (256, -1), (128, 0), (128, 0))
 PIECES = {(0, 0): ((512, 512), (512, 0)), (0, 1): ((512, 512), (512, 0)), (1, 0): ((512, 480), (512, 0)), (1, 1): ((512, 480), (256, 0), (128, 0)), (2, 0): ((512, 448), (512, 0)), (2, 1): ((512, 448), (256, 0), (128, 0)), (3, 0): ((512, 416), (256, 0), (128, 0))}
 G_PIECES = ((512, 512), (256, 0), (128, 0))
 BANK = 512

@@ -23,7 +23,7 @@ FLOPS = 2 * B * NPIX * K * C
 RUN = 8
 PIECE = 512
 VECTOR_COLS = (256, 240, 224, 208)
-TAIL_PIECES = ((256, 0), (256, 160), (256, -1), (128, 0), (128, 0))
+TAIL_PIECES = ((256, 0), (256, 96), (256, -1), (128, 0), (128, 0))
 PIECES = {(0, 0): ((512, 512), (512, 0)), (0, 1): ((512, 512), (512, 0)), (1, 0): ((512, 480), (512, 0)), (1, 1): ((512, 480), (256, 0), (128, 0)), (2, 0): ((512, 448), (512, 0)), (2, 1): ((512, 448), (256, 0), (128, 0)), (3, 0): ((512, 416), (256, 0), (128, 0))}
 G_PIECES = ((512, 512), (256, 0), (128, 0))
 BANK = 512

@@ -220,7 +220,7 @@ def tile_lvc_pb_kernel(tc, assign, xp, codebook, out):
                 )
                 if not SUM_ON_SCALAR:
                     nc.vector.tensor_copy(out=neg_sum[:, b : b + 1], in_=sums[:, b, 0:1])
-                for late in waiting:
+                for late in sorted(waiting, key=lambda w: w[2]):
                     product(*late)
                 waiting.clear()
                 return

from contextlib import ExitStack

import concourse.mybir as mybir
from concourse.masks import make_identity

FP8X4 = mybir.dt.float8_e4m3fn_x4
BF16 = mybir.dt.bfloat16
F32 = mybir.dt.float32
U32 = mybir.dt.uint32
U8 = mybir.dt.uint8

B = 4
NPIX = 1024
K = 128
C = 1024
P = 128
PACK = 4
PASSES = NPIX // (P * PACK)
ONES = 2

FLOPS = 2 * B * NPIX * K * C

RUN = 8
PIECE = 512
VECTOR_COLS = (256, 240, 224, 208)
TAIL_PIECES = ((256, 0), (256, 96), (256, -1), (128, 0), (128, 0))
PIECES = {(0, 0): ((512, 512), (512, 0)), (0, 1): ((512, 512), (512, 0)), (1, 0): ((512, 480), (512, 0)), (1, 1): ((512, 480), (256, 0), (128, 0)), (2, 0): ((512, 448), (512, 0)), (2, 1): ((512, 448), (256, 0), (128, 0)), (3, 0): ((512, 416), (256, 0), (128, 0))}
G_PIECES = ((512, 512), (256, 0), (128, 0))
BANK = 512
FINISH_LAG = 3
FIRST_FINISH_LAG = 4
LAST_FINISH_LAG = 3
STAGE_BUFS = 6
Q_LAG = 1
GPSIMD_COLS = 128
GPSIMD_CHUNKS = ((1, 1), (2, 1), (3, 0))
ONE_COPY = True
A_ON_SCALAR = True
ACC_BUFS = 6
R_BUFS = 1
R_ISSUE = ((("x", 3, 0, 512), ((3, 1, 512, 256),)),)
SUM_ON_SCALAR = True
ORDER = (("x", 0, 0), ("x", 0, 1), ("a", 0), ("x", 1, 0), ("x", 1, 1), ("a", 1), ("cb",), ("x", 2, 0), ("x", 2, 1), ("a", 2), ("a", 3), ("x", 3, 0), ("x", 3, 1))
LOAD_COLS = {}


def regroup(copy, dst, src):
    copy(
        out=dst.rearrange("p (c i) j -> p c j i", i=RUN),
        in_=src.rearrange("p j (c i) -> p c j i", i=RUN),
    )


def tile_lvc_pb_kernel(tc, assign, xp, codebook, out):
    nc = tc.nc
    with ExitStack() as ctx:
        raw = ctx.enter_context(tc.tile_pool(name="raw", bufs=1))
        stage = ctx.enter_context(tc.tile_pool(name="stage", bufs=STAGE_BUFS))
        keep = ctx.enter_context(tc.tile_pool(name="keep", bufs=1))
        ps_acc = ctx.enter_context(tc.psum_pool(name="ps_acc", bufs=ACC_BUFS))
        ps_sum = ctx.enter_context(tc.psum_pool(name="ps_sum", bufs=1))
        ps_r = ctx.enter_context(tc.psum_pool(name="ps_r", bufs=R_BUFS))
        ctx.enter_context(tc.manual_schedule())

        a_raw = {}
        x_raw = {}
        cb = raw.tile([P, C], BF16, name="cb")
        for item in ORDER:
            if item[0] == "cb":
                nc.sync.dma_start(out=cb[:], in_=codebook)
            elif item[0] == "a":
                b = item[1]
                t = raw.tile([P, PASSES, PACK, K], BF16, name="a_raw%d" % b)
                nc.sync.dma_start(
                    out=t[:],
                    in_=assign[b, :, :].rearrange("(c p j) k -> p c j k", c=PASSES, p=P, j=PACK),
                )
                a_raw[b] = t
            else:
                b, c = item[1], item[2]
                lw = LOAD_COLS.get((b, c), C)
                for w0 in range(0, C, lw):
                    t = raw.tile([P, PACK, lw], BF16, name="x_raw%d%d_%d" % (b, c, w0))
                    rows = xp[b, c * P * PACK : (c + 1) * P * PACK, w0 : w0 + lw]
                    nc.sync.dma_start(out=t[:], in_=rows.rearrange("(p j) w -> p j w", j=PACK))
                    x_raw[(b, c, w0)] = t

        ident = keep.tile([P, P], BF16, name="ident")
        make_identity(nc, ident[:])
        neg_ones = keep.tile([P, ONES], BF16, name="neg_ones")
        nc.vector.memset(neg_ones[:], -1.0)
        sums = ps_sum.tile([P, B, ONES], F32, name="sums")
        neg_sum = keep.tile([P, B], F32, name="neg_sum")

        steps = []
        for item in ORDER:
            if item[0] == "a":
                steps.append(("a", item[1], 0, 0, 0, 0))
            elif item[0] == "x":
                b, c = item[1], item[2]
                if b == B - 1 and c == PASSES - 1:
                    col0 = 0
                    for width, cut in TAIL_PIECES:
                        steps.append(("x" if cut >= 0 else "r", b, c, col0, width, max(cut, 0)))
                        col0 += width
                else:
                    col0 = 0
                    for width, cut in PIECES[(b, c)]:
                        steps.append(("x" if cut >= 0 else "r", b, c, col0, width, max(cut, 0)))
                        col0 += width
                    if (b, c) in GPSIMD_CHUNKS:
                        steps.append(("g", b, c, C - GPSIMD_COLS, GPSIMD_COLS, 0))

        def groups(b):
            if b < B - 1:
                return [(n0, BANK) for n0 in range(0, C, BANK)]
            found = []
            for width, cut in TAIL_PIECES:
                found.append((sum(w for n, w in found), width))
            return found

        grouped = {}
        a_codes = {}
        a_scales = {}
        x_codes = {}
        x_scales = {}
        acc = {}
        result = {}
        waiting = []

        r_bank = {}

        def tensor_regroup(b, c, col0, width):
            bank = ps_r.tile([P, width, PACK], BF16, name="rg")
            for w0 in range(0, width, P):
                nc.tensor.matmul(
                    out=bank[:, w0 : w0 + P, :],
                    lhsT=ident[:],
                    rhs=x_raw[(b, c, 0)][:, :, col0 + w0 : col0 + w0 + P].rearrange("p j w -> p w j"),
                    start=True,
                    stop=True,
                )
            r_bank[(b, c, col0)] = bank

        def do_regroup(i):
            kind, b, c, col0, width, cut = steps[i]
            for key, banks in R_ISSUE:
                if steps[i][:4] == key:
                    for bank in banks:
                        tensor_regroup(*bank)
            if kind == "g":
                return
            if kind == "r":
                g = stage.tile([P, width, PACK], BF16, name="gx", align_bytes=64)
                b0 = max(k[2] for k in r_bank if k[:2] == (b, c) and k[2] <= col0)
                nc.scalar.copy(out=g[:], in_=r_bank[(b, c, b0)][:, col0 - b0 : col0 - b0 + width, :])
                grouped[i] = g
                return
            if kind == "a":
                g = stage.tile([P, PASSES, K, PACK], BF16, name="ga", align_bytes=64)
                regroup(nc.scalar.copy if A_ON_SCALAR else nc.vector.tensor_copy, g[:, 0, :, :], a_raw[b][:, 0, :, :])
                regroup(nc.scalar.copy, g[:, 1, :, :], a_raw[b][:, 1, :, :])
                for r in range(PASSES * PACK):
                    nc.tensor.matmul(
                        out=sums[:, b, :],
                        lhsT=a_raw[b][:, r // PACK, r % PACK, :],
                        rhs=neg_ones[:],
                        start=(r == 0),
                        stop=(r == PASSES * PACK - 1),
                    )
                if SUM_ON_SCALAR:
                    nc.scalar.copy(out=neg_sum[:, b : b + 1], in_=sums[:, b, 0:1])
            else:
                g = stage.tile([P, width, PACK], BF16, name="gx", align_bytes=64)
                lw = LOAD_COLS.get((b, c), C)
                src = x_raw[(b, c, col0 - col0 % lw)]
                l0 = col0 % lw
                if cut > 0:
                    regroup(nc.vector.tensor_copy, g[:, 0:cut, :], src[:, :, l0 : l0 + cut])
                if cut < width:
                    regroup(nc.scalar.copy, g[:, cut:width, :], src[:, :, l0 + cut : l0 + width])
            grouped[i] = g

        def gpsimd_regroup(i, old):
            kind, b, c, col0, width, cut = steps[i]
            g = old[:, 0:width, :]
            nc.gpsimd.tensor_scalar(
                out=g,
                in0=x_raw[(b, c, 0)][:, :, col0 : col0 + width].rearrange("p j w -> p w j"),
                scalar1=1.0,
                scalar2=0.0,
                op0=mybir.AluOpType.mult,
                op1=mybir.AluOpType.add,
            )
            grouped[i] = g

        def product(b, c, n0, ns):
            if c == 0:
                acc[(b, n0)] = ps_acc.tile([P, ns], F32, name="acc")
            nc.tensor.matmul_mx(
                out=acc[(b, n0)][:],
                lhsT=a_codes[b][:, c * K : (c + 1) * K].bitcast(FP8X4),
                lhsT_scale=a_scales[b][:, c * K : (c + 1) * K],
                rhs=x_codes[(b, c)][:, n0 : n0 + ns].bitcast(FP8X4),
                rhs_scale=x_scales[(b, c)][:, n0 : n0 + ns],
                start=(c == 0),
                stop=(c == PASSES - 1),
            )

        def do_multiply(i):
            kind, b, c, col0, width, cut = steps[i]
            g = grouped[i]
            if kind == "a":
                a_codes[b] = keep.tile([P, PASSES * K], U32, name="a_codes%d" % b, align_bytes=64)
                a_scales[b] = keep.tile([P, PASSES * K], U8, name="a_scales%d" % b, align_bytes=64)
                nc.vector.quantize_mx(
                    out=a_codes[b][:].bitcast(FP8X4),
                    scales=a_scales[b][:],
                    in_=g[:].rearrange("p c k j -> p (c k j)"),
                )
                if not SUM_ON_SCALAR:
                    nc.vector.tensor_copy(out=neg_sum[:, b : b + 1], in_=sums[:, b, 0:1])
                for late in sorted(waiting, key=lambda w: w[2]):
                    product(*late)
                waiting.clear()
                return
            if col0 == 0:
                x_codes[(b, c)] = keep.tile([P, C], U32, name="x_codes%d%d" % (b, c), align_bytes=64)
                x_scales[(b, c)] = keep.tile([P, C], U8, name="x_scales%d%d" % (b, c), align_bytes=64)
            nc.vector.quantize_mx(
                out=x_codes[(b, c)][:, col0 : col0 + width].bitcast(FP8X4),
                scales=x_scales[(b, c)][:, col0 : col0 + width],
                in_=g.rearrange("p w j -> p (w j)") if kind == "g" else g[:].rearrange("p w j -> p (w j)"),
            )
            for n0, ns in [g for g in groups(b) if col0 < g[0] + g[1] <= col0 + width]:
                if b in a_codes:
                    product(b, c, n0, ns)
                else:
                    waiting.append((b, c, n0, ns))

        def do_finish(i):
            kind, b, c, col0, width, cut = steps[i]
            if col0 == 0:
                result[b] = keep.tile([P, C], F32, name="result%d" % b)
            for n0, ns in [g for g in groups(b) if col0 < g[0] + g[1] <= col0 + width]:
                nc.vector.scalar_tensor_tensor(
                    out=result[b][:, n0 : n0 + ns],
                    in0=cb[:, n0 : n0 + ns],
                    scalar=neg_sum[:, b : b + 1],
                    in1=acc[(b, n0)][:],
                    op0=mybir.AluOpType.mult,
                    op1=mybir.AluOpType.add,
                )
                nc.sync.dma_start(out=out[b, :, n0 : n0 + ns], in_=result[b][:, n0 : n0 + ns])

        finish_at = {}
        for i in range(len(steps)):
            if steps[i][0] in ("x", "g", "r") and steps[i][2] == PASSES - 1:
                lag = FIRST_FINISH_LAG if steps[i][1] == 0 else (LAST_FINISH_LAG if steps[i][1] == B - 1 else FINISH_LAG)
                last = max(s for s in range(len(steps)) if steps[s][1] == steps[i][1] and steps[s][0] != "a")
                at = max(i if steps[i][1] == B - 1 else last, steps.index(("a", steps[i][1], 0, 0, 0, 0))) + lag
                finish_at[at] = finish_at.get(at, []) + [i]
        for i in range(len(steps) + LAST_FINISH_LAG + Q_LAG):
            if i < len(steps):
                do_regroup(i)
            if 0 <= i - Q_LAG < len(steps):
                do_multiply(i - Q_LAG)
            due = finish_at.get(i - Q_LAG + 1, [])
            if due and steps[due[0]][1] < B - 1:
                later = [s for s in range(i, len(steps)) if steps[s][0] == "g"]
                if later and GPSIMD_COLS:
                    gpsimd_regroup(later[0], grouped[i - Q_LAG])
            for j in due:
                do_finish(j)
